import numpy as np
import ml_dtypes


def mxq(x, axis, fmt="e4m3"):
    dtype, down = {"e4m3": (ml_dtypes.float8_e4m3fn, 7), "e5m2": (ml_dtypes.float8_e5m2, 14)}[fmt]
    v = np.moveaxis(np.asarray(x, np.float32).astype(ml_dtypes.bfloat16).astype(np.float64), axis, -1)
    blocks = v.reshape(v.shape[:-1] + (-1, 32))
    amax = np.abs(blocks).max(-1, keepdims=True)
    byte = np.maximum(np.where(amax > 0, np.frexp(amax)[1] - 1 + 127, 0) - down, 1)
    scale = np.exp2(byte - 127.0)
    codes = (blocks / scale).astype(np.float32).astype(dtype).astype(np.float64)
    return np.moveaxis((codes * scale).reshape(v.shape), -1, axis)


WIDE = False


def mx_kscale(k):
    if not WIDE:
        return np.ones(k)
    levels = np.array([20, -20, 10, -10, 0])
    a = np.random.permutation(np.resize(levels, k // 512 * 4)).reshape(k // 512, 4)
    idx = np.arange(k)
    return np.exp2(a[idx // 512, idx % 128 // 32])


BF16 = ml_dtypes.bfloat16


def bf(x):
    return np.asarray(x, np.float32).astype(BF16)


def f64(x):
    return np.asarray(x).astype(np.float64)


B, D, H = 2048, 1024, 512


def pre_activation(h_c1, h_c2, x_t, r_param, theta_param, w1, w2):
    h_c1, h_c2, x_t = f64(h_c1), f64(h_c2), f64(x_t)
    r, theta = f64(r_param), f64(theta_param)
    g = r * np.cos(theta)
    phi = r * np.sin(theta)
    norm = np.sqrt(np.maximum(1.0 - r * r, 0.0))
    h_t_c1 = g * h_c1 - phi * h_c2 + norm * (x_t @ f64(w1))
    h_t_c2 = g * h_c2 + phi * h_c1 + norm * (x_t @ f64(w2))
    return np.concatenate((h_t_c1, h_t_c2), axis=-1)


def setup_inputs():
    u = mx_kscale(H)
    h_c1 = bf(np.random.standard_normal((B, H)))
    h_c2 = bf(np.random.standard_normal((B, H)))
    x_t = bf(np.random.standard_normal((B, D)))
    r_param = bf(np.random.uniform(0.1, 1.05, (1, H)))
    theta_param = bf(np.random.uniform(0.0, 2.0 * np.pi, (1, H)))
    w10 = bf(np.random.standard_normal((D, H)) / np.sqrt(D))
    w20 = bf(np.random.standard_normal((D, H)) / np.sqrt(D))
    g = bf(np.random.standard_normal((B, 2 * H)) * np.exp2(np.random.randint(-12, 1, (B, 1))) * 16.0 * np.concatenate((u, u)))
    z = pre_activation(h_c1, h_c2, x_t, r_param, theta_param, w10, w20)
    return {"h_c1": h_c1, "h_c2": h_c2, "x_t": x_t, "r_param": r_param, "theta_param": theta_param,
            "w1": bf(f64(w10) / u), "w2": bf(f64(w20) / u),
            "z": np.asarray(z, np.float32), "grad_out": g}


def reference(h_c1, h_c2, x_t, r_param, theta_param, w1, w2, z, grad_out):
    r = f64(r_param)
    norm = np.sqrt(np.maximum(1.0 - r * r, 0.0))
    dz = f64(grad_out) * (f64(z) > 0.0) * np.concatenate((norm, norm), axis=1)
    d1 = mxq(dz[:, :H], 1, "e5m2")
    d2 = mxq(dz[:, H:], 1, "e5m2")
    p1 = d1 @ mxq(f64(w1), 1, "e4m3").T
    p2 = d2 @ mxq(f64(w2), 1, "e4m3").T
    return p1 + p2

@@ -1,0 +1,195 @@
+from contextlib import ExitStack
+
+import concourse.mybir as mybir
+from concourse.masks import make_identity
+
+F32 = mybir.dt.float32
+BF16 = mybir.dt.bfloat16
+U32 = mybir.dt.uint32
+U8 = mybir.dt.uint8
+E4M3_X4 = mybir.dt.float8_e4m3fn_x4
+E5M2_X4 = mybir.dt.float8_e5m2_x4
+ALU = mybir.AluOpType
+ACT = mybir.ActivationFunctionType
+
+P = 128
+TOKENS, D_IN, HIDDEN = 2048, 1024, 512
+HALVES = 2
+PLANES = 2
+PAIR = 2
+PACK = PLANES * PAIR
+WORDS = HIDDEN // PAIR
+TOKEN_TILES = TOKENS // P
+N_MOVING = 512
+COLUMN_BLOCKS = D_IN // N_MOVING
+QUARTERS = HALVES * COLUMN_BLOCKS
+ROWS_TOGETHER = 2
+SQRT_FLOOR = 2.0**-100
+
+FLOPS = 2 * TOKENS * D_IN * HALVES * HIDDEN
+BYTES = 2 * HIDDEN + 2 * HALVES * D_IN * HIDDEN + (4 + 2) * TOKENS * HALVES * HIDDEN + 4 * TOKENS * D_IN
+
+
+def tile_linearrtus_t_v_kernel(
+    tc, h_c1, h_c2, x_t, r_param, theta_param, w1, w2, z, grad_out, out
+):
+    nc = tc.nc
+    weights = (w1, w2)
+    z_tiles = z.rearrange("(p t) k -> p t k", t=TOKEN_TILES)
+    grad_tiles = grad_out.rearrange("(p t) k -> p t k", t=TOKEN_TILES)
+    out_tiles = out.rearrange("(p t) d -> p t d", t=TOKEN_TILES)
+
+    with ExitStack() as pools:
+        const = pools.enter_context(tc.tile_pool(name="const", bufs=1))
+        loaded = pools.enter_context(tc.tile_pool(name="loaded", bufs=1))
+        w_keep = pools.enter_context(tc.tile_pool(name="w_keep", bufs=1))
+        w_work = pools.enter_context(tc.tile_pool(name="w_work", bufs=2))
+        dz_work = pools.enter_context(tc.tile_pool(name="dz_work", bufs=3))
+        dz_keep = pools.enter_context(tc.tile_pool(name="dz_keep", bufs=6))
+        results = pools.enter_context(tc.tile_pool(name="results", bufs=4))
+        turned_banks = pools.enter_context(tc.psum_pool(name="turned_banks", bufs=4))
+        sum_banks = pools.enter_context(tc.psum_pool(name="sum_banks", bufs=4))
+
+        z_of, grad_of, w_rows = {}, {}, {}
+
+        def load_tokens(first, count):
+            grad_sb = loaded.tile([P, count, HALVES * HIDDEN], BF16, name="grad%d" % first)
+            z_sb = loaded.tile([P, count, HALVES * HIDDEN], F32, name="z%d" % first)
+            nc.sync.dma_start(out=grad_sb[:], in_=grad_tiles[:, first : first + count, :])
+            nc.sync.dma_start(out=z_sb[:], in_=z_tiles[:, first : first + count, :])
+            for n in range(count):
+                grad_of[first + n] = grad_sb[:, n, :]
+                z_of[first + n] = z_sb[:, n, :]
+
+        def load_weight_quarter(quarter):
+            block, half = divmod(quarter, HALVES)
+            rows = weights[half][block * N_MOVING : (block + 1) * N_MOVING, :]
+            w_sb = loaded.tile(
+                [P, N_MOVING // (P * ROWS_TOGETHER), ROWS_TOGETHER, HIDDEN], BF16, name="w%d" % quarter
+            )
+            nc.sync.dma_start(
+                out=w_sb[:], in_=rows.rearrange("(j c i) k -> c j i k", c=P, i=ROWS_TOGETHER)
+            )
+            w_rows[quarter] = w_sb
+
+        r_sb = const.tile([P, PACK], BF16)
+        nc.scalar.dma_start(
+            out=r_sb[:].rearrange("p (u e) -> p u e", e=PAIR),
+            in_=r_param.rearrange("o (u p e) -> p (o u) e", u=PLANES, e=PAIR),
+        )
+        for quarter in range(QUARTERS):
+            load_tokens(quarter, 1)
+            load_weight_quarter(quarter)
+        for first in range(QUARTERS, TOKEN_TILES, 2):
+            load_tokens(first, 2)
+
+        identity = const.tile([P, P], F32)
+        make_identity(nc, identity[:])
+
+        r_squared = const.tile([P, PACK], F32)
+        nc.vector.tensor_tensor(out=r_squared[:], in0=r_sb[:], in1=r_sb[:], op=ALU.mult)
+        one_minus = const.tile([P, PACK], F32)
+        nc.vector.tensor_scalar(
+            out=one_minus[:], in0=r_squared[:], scalar1=-1.0, scalar2=1.0, op0=ALU.mult, op1=ALU.add
+        )
+        floored = const.tile([P, PACK], F32)
+        nc.vector.tensor_scalar_max(out=floored[:], in0=one_minus[:], scalar1=SQRT_FLOOR)
+        root = const.tile([P, PACK], F32)
+        nc.scalar.activation(out=root[:], in_=floored[:], func=ACT.Sqrt)
+        norm = const.tile([P, PACK], F32)
+        nc.vector.scalar_tensor_tensor(
+            out=norm[:], in0=one_minus[:], scalar=0.0, in1=root[:], op0=ALU.is_gt, op1=ALU.mult
+        )
+        norm_for_all_tokens = (
+            norm[:]
+            .rearrange("p (u e) -> p u e", e=PAIR)
+            .unsqueeze(1)
+            .to_broadcast([P, HALVES * P, PLANES, PAIR])
+        )
+
+        w_codes, w_scales = {}, {}
+
+        def prepare_weight_quarter(quarter):
+            grouped = w_work.tile([P, N_MOVING * PACK], BF16, name="w_grouped", align_bytes=64)
+            grouped_words = grouped[:].bitcast(F32)
+            per_bank = P * ROWS_TOGETHER
+            for j in range(N_MOVING // per_bank):
+                turned = turned_banks.tile([P, PLANES * per_bank], F32, name="turned", tag="turned")
+                for u in range(PLANES):
+                    for i in range(ROWS_TOGETHER):
+                        row_words = w_rows[quarter][:, j, i, :].bitcast(F32)
+                        nc.tensor.transpose(
+                            turned[:, (u * ROWS_TOGETHER + i) * P : (u * ROWS_TOGETHER + i + 1) * P],
+                            row_words[:, u * P : (u + 1) * P],
+                            identity[:],
+                        )
+                nc.scalar.copy(
+                    out=grouped_words[:, j * per_bank * PLANES : (j + 1) * per_bank * PLANES].rearrange(
+                        "p (c i u) -> p c i u", i=ROWS_TOGETHER, u=PLANES
+                    ),
+                    in_=turned[:].rearrange("p (u i c) -> p c i u", u=PLANES, i=ROWS_TOGETHER),
+                )
+            codes = w_keep.tile([P, N_MOVING], U32, name="w_codes%d" % quarter, align_bytes=64)
+            scales = w_keep.tile([P, N_MOVING], U8, name="w_scales%d" % quarter, align_bytes=64)
+            nc.vector.quantize_mx(out=codes[:].bitcast(E4M3_X4), scales=scales[:], in_=grouped[:])
+            w_codes[quarter], w_scales[quarter] = codes, scales
+
+        dz_codes, dz_scales = {}, {}
+
+        def make_dz(t):
+            masked = dz_work.tile([P, HALVES * HIDDEN], BF16)
+            nc.vector.scalar_tensor_tensor(
+                out=masked[:], in0=z_of[t], scalar=0.0, in1=grad_of[t], op0=ALU.is_gt, op1=ALU.mult
+            )
+            masked_words = masked[:].bitcast(F32)
+            turned = turned_banks.tile([P, PLANES * HALVES * P], F32, name="turned", tag="turned")
+            for u in range(PLANES):
+                for half in range(HALVES):
+                    nc.tensor.transpose(
+                        turned[:, (u * HALVES + half) * P : (u * HALVES + half + 1) * P],
+                        masked_words[:, half * WORDS + u * P : half * WORDS + (u + 1) * P],
+                        identity[:],
+                    )
+            grouped = dz_work.tile([P, HALVES * P, PLANES, PAIR], BF16, align_bytes=64)
+            nc.vector.tensor_tensor(
+                out=grouped[:],
+                in0=turned[:].bitcast(BF16).rearrange("p (u c e) -> p c u e", u=PLANES, e=PAIR),
+                in1=norm_for_all_tokens,
+                op=ALU.mult,
+            )
+            codes = dz_keep.tile([P, HALVES * P], U32, name="dz_codes", align_bytes=64)
+            scales = dz_keep.tile([P, HALVES * P], U8, name="dz_scales", align_bytes=64)
+            nc.vector.quantize_mx(
+                out=codes[:].bitcast(E5M2_X4),
+                scales=scales[:],
+                in_=grouped[:].rearrange("p c u e -> p (c u e)"),
+            )
+            dz_codes[t], dz_scales[t] = codes, scales
+
+        def multiply(t):
+            result = results.tile([P, D_IN], F32)
+            for block in range(COLUMN_BLOCKS):
+                sums = sum_banks.tile([P, N_MOVING], F32)
+                for half in range(HALVES):
+                    quarter = block * HALVES + half
+                    tokens = slice(half * P, (half + 1) * P)
+                    nc.tensor.matmul_mx(
+                        out=sums[:],
+                        lhsT=dz_codes[t][:, tokens].bitcast(E5M2_X4),
+                        lhsT_scale=dz_scales[t][:, tokens],
+                        rhs=w_codes[quarter][:].bitcast(E4M3_X4),
+                        rhs_scale=w_scales[quarter][:],
+                        start=(half == 0),
+                        stop=(half == HALVES - 1),
+                    )
+                nc.scalar.copy(out=result[:, block * N_MOVING : (block + 1) * N_MOVING], in_=sums[:])
+            nc.scalar.dma_start(out=out_tiles[:, t, :], in_=result[:])
+
+        for t in range(QUARTERS):
+            make_dz(t)
+            prepare_weight_quarter(t)
+        for t in range(QUARTERS):
+            multiply(t)
+        for t in range(QUARTERS, TOKEN_TILES):
+            make_dz(t)
+            multiply(t)

@@ -24,6 +24,7 @@ N_MOVING = 512
 COLUMN_BLOCKS = D_IN // N_MOVING
 QUARTERS = HALVES * COLUMN_BLOCKS
 ROWS_TOGETHER = 2
+RESULT_BUFFERS = 10
 SQRT_FLOOR = 2.0**-100
 
 FLOPS = 2 * TOKENS * D_IN * HALVES * HIDDEN
@@ -46,7 +47,7 @@ def tile_linearrtus_t_v_kernel(
         w_work = pools.enter_context(tc.tile_pool(name="w_work", bufs=2))
         dz_work = pools.enter_context(tc.tile_pool(name="dz_work", bufs=3))
         dz_keep = pools.enter_context(tc.tile_pool(name="dz_keep", bufs=6))
-        results = pools.enter_context(tc.tile_pool(name="results", bufs=4))
+        results = pools.enter_context(tc.tile_pool(name="results", bufs=RESULT_BUFFERS))
         turned_banks = pools.enter_context(tc.psum_pool(name="turned_banks", bufs=4))
         sum_banks = pools.enter_context(tc.psum_pool(name="sum_banks", bufs=4))
 
@@ -80,8 +81,10 @@ def tile_linearrtus_t_v_kernel(
         for quarter in range(QUARTERS):
             load_tokens(quarter, 1)
             load_weight_quarter(quarter)
-        for first in range(QUARTERS, TOKEN_TILES, 2):
+        for first in range(QUARTERS, TOKEN_TILES // 2, 2):
             load_tokens(first, 2)
+        for first in range(TOKEN_TILES // 2, TOKEN_TILES, 4):
+            load_tokens(first, 4)
 
         identity = const.tile([P, P], F32)
         make_identity(nc, identity[:])
@@ -183,7 +186,7 @@ def tile_linearrtus_t_v_kernel(
                         stop=(half == HALVES - 1),
                     )
                 nc.scalar.copy(out=result[:, block * N_MOVING : (block + 1) * N_MOVING], in_=sums[:])
-            nc.scalar.dma_start(out=out_tiles[:, t, :], in_=result[:])
+            nc.sync.dma_start(out=out_tiles[:, t, :], in_=result[:])
 
         for t in range(QUARTERS):
             make_dz(t)

@@ -24,7 +24,6 @@ N_MOVING = 512
 COLUMN_BLOCKS = D_IN // N_MOVING
 QUARTERS = HALVES * COLUMN_BLOCKS
 ROWS_TOGETHER = 2
-RESULT_BUFFERS = 10
 SQRT_FLOOR = 2.0**-100
 
 FLOPS = 2 * TOKENS * D_IN * HALVES * HIDDEN
@@ -41,14 +40,16 @@ def tile_linearrtus_t_v_kernel(
     out_tiles = out.rearrange("(p t) d -> p t d", t=TOKEN_TILES)
 
     with ExitStack() as pools:
+        pools.enter_context(tc.manual_schedule())
         const = pools.enter_context(tc.tile_pool(name="const", bufs=1))
         loaded = pools.enter_context(tc.tile_pool(name="loaded", bufs=1))
         w_keep = pools.enter_context(tc.tile_pool(name="w_keep", bufs=1))
         w_work = pools.enter_context(tc.tile_pool(name="w_work", bufs=2))
         dz_work = pools.enter_context(tc.tile_pool(name="dz_work", bufs=3))
         dz_keep = pools.enter_context(tc.tile_pool(name="dz_keep", bufs=6))
-        results = pools.enter_context(tc.tile_pool(name="results", bufs=RESULT_BUFFERS))
-        turned_banks = pools.enter_context(tc.psum_pool(name="turned_banks", bufs=4))
+        results = pools.enter_context(tc.tile_pool(name="results", bufs=4))
+        w_banks = pools.enter_context(tc.psum_pool(name="w_banks", bufs=2))
+        dz_banks = pools.enter_context(tc.psum_pool(name="dz_banks", bufs=2))
         sum_banks = pools.enter_context(tc.psum_pool(name="sum_banks", bufs=4))
 
         z_of, grad_of, w_rows = {}, {}, {}
@@ -81,10 +82,8 @@ def tile_linearrtus_t_v_kernel(
         for quarter in range(QUARTERS):
             load_tokens(quarter, 1)
             load_weight_quarter(quarter)
-        for first in range(QUARTERS, TOKEN_TILES // 2, 2):
+        for first in range(QUARTERS, TOKEN_TILES, 2):
             load_tokens(first, 2)
-        for first in range(TOKEN_TILES // 2, TOKEN_TILES, 4):
-            load_tokens(first, 4)
 
         identity = const.tile([P, P], F32)
         make_identity(nc, identity[:])
@@ -110,14 +109,14 @@ def tile_linearrtus_t_v_kernel(
             .to_broadcast([P, HALVES * P, PLANES, PAIR])
         )
 
-        w_codes, w_scales = {}, {}
+        w_grouped, w_codes, w_scales = {}, {}, {}
 
-        def prepare_weight_quarter(quarter):
+        def turn_weight_quarter(quarter):
             grouped = w_work.tile([P, N_MOVING * PACK], BF16, name="w_grouped", align_bytes=64)
             grouped_words = grouped[:].bitcast(F32)
             per_bank = P * ROWS_TOGETHER
             for j in range(N_MOVING // per_bank):
-                turned = turned_banks.tile([P, PLANES * per_bank], F32, name="turned", tag="turned")
+                turned = w_banks.tile([P, PLANES * per_bank], F32, name="w_turned")
                 for u in range(PLANES):
                     for i in range(ROWS_TOGETHER):
                         row_words = w_rows[quarter][:, j, i, :].bitcast(F32)
@@ -132,20 +131,25 @@ def tile_linearrtus_t_v_kernel(
                     ),
                     in_=turned[:].rearrange("p (u i c) -> p c i u", u=PLANES, i=ROWS_TOGETHER),
                 )
+            w_grouped[quarter] = grouped
+
+        def quantise_weight_quarter(quarter):
             codes = w_keep.tile([P, N_MOVING], U32, name="w_codes%d" % quarter, align_bytes=64)
             scales = w_keep.tile([P, N_MOVING], U8, name="w_scales%d" % quarter, align_bytes=64)
-            nc.vector.quantize_mx(out=codes[:].bitcast(E4M3_X4), scales=scales[:], in_=grouped[:])
+            nc.vector.quantize_mx(
+                out=codes[:].bitcast(E4M3_X4), scales=scales[:], in_=w_grouped[quarter][:]
+            )
             w_codes[quarter], w_scales[quarter] = codes, scales
 
-        dz_codes, dz_scales = {}, {}
+        dz_turned, dz_grouped, dz_codes, dz_scales = {}, {}, {}, {}
 
-        def make_dz(t):
+        def mask_and_turn(t):
             masked = dz_work.tile([P, HALVES * HIDDEN], BF16)
             nc.vector.scalar_tensor_tensor(
                 out=masked[:], in0=z_of[t], scalar=0.0, in1=grad_of[t], op0=ALU.is_gt, op1=ALU.mult
             )
             masked_words = masked[:].bitcast(F32)
-            turned = turned_banks.tile([P, PLANES * HALVES * P], F32, name="turned", tag="turned")
+            turned = dz_banks.tile([P, PLANES * HALVES * P], F32, name="dz_turned")
             for u in range(PLANES):
                 for half in range(HALVES):
                     nc.tensor.transpose(
@@ -153,19 +157,25 @@ def tile_linearrtus_t_v_kernel(
                         masked_words[:, half * WORDS + u * P : half * WORDS + (u + 1) * P],
                         identity[:],
                     )
+            dz_turned[t] = turned
+
+        def scale_by_norm(t):
             grouped = dz_work.tile([P, HALVES * P, PLANES, PAIR], BF16, align_bytes=64)
             nc.vector.tensor_tensor(
                 out=grouped[:],
-                in0=turned[:].bitcast(BF16).rearrange("p (u c e) -> p c u e", u=PLANES, e=PAIR),
+                in0=dz_turned[t][:].bitcast(BF16).rearrange("p (u c e) -> p c u e", u=PLANES, e=PAIR),
                 in1=norm_for_all_tokens,
                 op=ALU.mult,
             )
+            dz_grouped[t] = grouped
+
+        def quantise_dz(t):
             codes = dz_keep.tile([P, HALVES * P], U32, name="dz_codes", align_bytes=64)
             scales = dz_keep.tile([P, HALVES * P], U8, name="dz_scales", align_bytes=64)
             nc.vector.quantize_mx(
                 out=codes[:].bitcast(E5M2_X4),
                 scales=scales[:],
-                in_=grouped[:].rearrange("p c u e -> p (c u e)"),
+                in_=dz_grouped[t][:].rearrange("p c u e -> p (c u e)"),
             )
             dz_codes[t], dz_scales[t] = codes, scales
 
@@ -186,13 +196,19 @@ def tile_linearrtus_t_v_kernel(
                         stop=(half == HALVES - 1),
                     )
                 nc.scalar.copy(out=result[:, block * N_MOVING : (block + 1) * N_MOVING], in_=sums[:])
-            nc.sync.dma_start(out=out_tiles[:, t, :], in_=result[:])
+            nc.scalar.dma_start(out=out_tiles[:, t, :], in_=result[:])
 
-        for t in range(QUARTERS):
-            make_dz(t)
-            prepare_weight_quarter(t)
-        for t in range(QUARTERS):
-            multiply(t)
-        for t in range(QUARTERS, TOKEN_TILES):
-            make_dz(t)
-            multiply(t)
+        for step in range(TOKEN_TILES + 2):
+            if step < TOKEN_TILES:
+                mask_and_turn(step)
+            if step < QUARTERS:
+                turn_weight_quarter(step)
+            if 1 <= step <= QUARTERS:
+                quantise_weight_quarter(step - 1)
+            if step >= 2:
+                quantise_dz(step - 2)
+            if 1 <= step <= TOKEN_TILES:
+                scale_by_norm(step - 1)
+            if step >= QUARTERS:
+                for t in range(0 if step == QUARTERS else step - 2, step - 1):
+                    multiply(t)

@@ -24,6 +24,8 @@ N_MOVING = 512
 COLUMN_BLOCKS = D_IN // N_MOVING
 QUARTERS = HALVES * COLUMN_BLOCKS
 ROWS_TOGETHER = 2
+SCALAR_EVERY = 4
+PRODUCTS_A_STEP = 2
 SQRT_FLOOR = 2.0**-100
 
 FLOPS = 2 * TOKENS * D_IN * HALVES * HIDDEN
@@ -48,9 +50,8 @@ def tile_linearrtus_t_v_kernel(
         dz_work = pools.enter_context(tc.tile_pool(name="dz_work", bufs=3))
         dz_keep = pools.enter_context(tc.tile_pool(name="dz_keep", bufs=6))
         results = pools.enter_context(tc.tile_pool(name="results", bufs=4))
-        w_banks = pools.enter_context(tc.psum_pool(name="w_banks", bufs=2))
         dz_banks = pools.enter_context(tc.psum_pool(name="dz_banks", bufs=2))
-        sum_banks = pools.enter_context(tc.psum_pool(name="sum_banks", bufs=4))
+        banks = pools.enter_context(tc.psum_pool(name="banks", bufs=6))
 
         z_of, grad_of, w_rows = {}, {}, {}
 
@@ -116,7 +117,7 @@ def tile_linearrtus_t_v_kernel(
             grouped_words = grouped[:].bitcast(F32)
             per_bank = P * ROWS_TOGETHER
             for j in range(N_MOVING // per_bank):
-                turned = w_banks.tile([P, PLANES * per_bank], F32, name="w_turned")
+                turned = banks.tile([P, PLANES * per_bank], F32, name="w_turned", tag="bank")
                 for u in range(PLANES):
                     for i in range(ROWS_TOGETHER):
                         row_words = w_rows[quarter][:, j, i, :].bitcast(F32)
@@ -159,14 +160,23 @@ def tile_linearrtus_t_v_kernel(
                     )
             dz_turned[t] = turned
 
+        def scalar_scales(t):
+            return t > QUARTERS and t % SCALAR_EVERY == 1
+
         def scale_by_norm(t):
             grouped = dz_work.tile([P, HALVES * P, PLANES, PAIR], BF16, align_bytes=64)
-            nc.vector.tensor_tensor(
-                out=grouped[:],
-                in0=dz_turned[t][:].bitcast(BF16).rearrange("p (u c e) -> p c u e", u=PLANES, e=PAIR),
-                in1=norm_for_all_tokens,
-                op=ALU.mult,
-            )
+            values = dz_turned[t][:].bitcast(BF16).rearrange("p (u c e) -> p c u e", u=PLANES, e=PAIR)
+            if scalar_scales(t):
+                for u in range(PLANES):
+                    for e in range(PAIR):
+                        nc.scalar.activation(
+                            out=grouped[:, :, u, e],
+                            in_=values[:, :, u, e],
+                            func=ACT.Copy,
+                            scale=norm[:, u * PAIR + e : u * PAIR + e + 1],
+                        )
+            else:
+                nc.vector.tensor_tensor(out=grouped[:], in0=values, in1=norm_for_all_tokens, op=ALU.mult)
             dz_grouped[t] = grouped
 
         def quantise_dz(t):
@@ -182,7 +192,7 @@ def tile_linearrtus_t_v_kernel(
         def multiply(t):
             result = results.tile([P, D_IN], F32)
             for block in range(COLUMN_BLOCKS):
-                sums = sum_banks.tile([P, N_MOVING], F32)
+                sums = banks.tile([P, N_MOVING], F32, name="sums", tag="bank")
                 for half in range(HALVES):
                     quarter = block * HALVES + half
                     tokens = slice(half * P, (half + 1) * P)
@@ -198,17 +208,22 @@ def tile_linearrtus_t_v_kernel(
                 nc.scalar.copy(out=result[:, block * N_MOVING : (block + 1) * N_MOVING], in_=sums[:])
             nc.scalar.dma_start(out=out_tiles[:, t, :], in_=result[:])
 
+        waiting = []
         for step in range(TOKEN_TILES + 2):
             if step < TOKEN_TILES:
                 mask_and_turn(step)
+                if scalar_scales(step):
+                    scale_by_norm(step)
             if step < QUARTERS:
                 turn_weight_quarter(step)
             if 1 <= step <= QUARTERS:
                 quantise_weight_quarter(step - 1)
             if step >= 2:
                 quantise_dz(step - 2)
-            if 1 <= step <= TOKEN_TILES:
+                waiting.append(step - 2)
+            if 1 <= step <= TOKEN_TILES and not scalar_scales(step - 1):
                 scale_by_norm(step - 1)
             if step >= QUARTERS:
-                for t in range(0 if step == QUARTERS else step - 2, step - 1):
+                for t in waiting[:PRODUCTS_A_STEP]:
                     multiply(t)
+                waiting = waiting[PRODUCTS_A_STEP:]

@@ -26,6 +26,7 @@ QUARTERS = HALVES * COLUMN_BLOCKS
 ROWS_TOGETHER = 2
 SCALAR_EVERY = 4
 PRODUCTS_A_STEP = 2
+RESULT_BUFFERS = 12
 SQRT_FLOOR = 2.0**-100
 
 FLOPS = 2 * TOKENS * D_IN * HALVES * HIDDEN
@@ -47,9 +48,9 @@ def tile_linearrtus_t_v_kernel(
         loaded = pools.enter_context(tc.tile_pool(name="loaded", bufs=1))
         w_keep = pools.enter_context(tc.tile_pool(name="w_keep", bufs=1))
         w_work = pools.enter_context(tc.tile_pool(name="w_work", bufs=2))
-        dz_work = pools.enter_context(tc.tile_pool(name="dz_work", bufs=3))
+        dz_work = pools.enter_context(tc.tile_pool(name="dz_work", bufs=4))
         dz_keep = pools.enter_context(tc.tile_pool(name="dz_keep", bufs=6))
-        results = pools.enter_context(tc.tile_pool(name="results", bufs=4))
+        results = pools.enter_context(tc.tile_pool(name="results", bufs=RESULT_BUFFERS))
         dz_banks = pools.enter_context(tc.psum_pool(name="dz_banks", bufs=2))
         banks = pools.enter_context(tc.psum_pool(name="banks", bufs=6))
 
@@ -80,11 +81,13 @@ def tile_linearrtus_t_v_kernel(
             out=r_sb[:].rearrange("p (u e) -> p u e", e=PAIR),
             in_=r_param.rearrange("o (u p e) -> p (o u) e", u=PLANES, e=PAIR),
         )
+        load_tokens(0, 1)
         for quarter in range(QUARTERS):
-            load_tokens(quarter, 1)
+            load_tokens(quarter + 1, 1)
             load_weight_quarter(quarter)
-        for first in range(QUARTERS, TOKEN_TILES, 2):
+        for first in range(QUARTERS + 1, TOKEN_TILES - 1, 2):
             load_tokens(first, 2)
+        load_tokens(TOKEN_TILES - 1, 1)
 
         identity = const.tile([P, P], F32)
         make_identity(nc, identity[:])
@@ -206,7 +209,10 @@ def tile_linearrtus_t_v_kernel(
                         stop=(half == HALVES - 1),
                     )
                 nc.scalar.copy(out=result[:, block * N_MOVING : (block + 1) * N_MOVING], in_=sums[:])
-            nc.scalar.dma_start(out=out_tiles[:, t, :], in_=result[:])
+            nc.sync.dma_start(out=out_tiles[:, t, :], in_=result[:])
+
+        def steps_to_quantise(t):
+            return 3 if scalar_scales(t) else 2
 
         waiting = []
         for step in range(TOKEN_TILES + 2):
@@ -214,16 +220,17 @@ def tile_linearrtus_t_v_kernel(
                 mask_and_turn(step)
                 if scalar_scales(step):
                     scale_by_norm(step)
-            if step < QUARTERS:
-                turn_weight_quarter(step)
             if 1 <= step <= QUARTERS:
-                quantise_weight_quarter(step - 1)
-            if step >= 2:
-                quantise_dz(step - 2)
-                waiting.append(step - 2)
+                turn_weight_quarter(step - 1)
+            if 2 <= step <= QUARTERS + 1:
+                quantise_weight_quarter(step - 2)
+            for t in (step - 3, step - 2):
+                if 0 <= t < TOKEN_TILES and step - t == steps_to_quantise(t):
+                    quantise_dz(t)
+                    waiting.append(t)
             if 1 <= step <= TOKEN_TILES and not scalar_scales(step - 1):
                 scale_by_norm(step - 1)
-            if step >= QUARTERS:
+            if step > QUARTERS:
                 for t in waiting[:PRODUCTS_A_STEP]:
                     multiply(t)
                 waiting = waiting[PRODUCTS_A_STEP:]

@@ -24,9 +24,9 @@ N_MOVING = 512
 COLUMN_BLOCKS = D_IN // N_MOVING
 QUARTERS = HALVES * COLUMN_BLOCKS
 ROWS_TOGETHER = 2
-SCALAR_EVERY = 4
-PRODUCTS_A_STEP = 2
-RESULT_BUFFERS = 12
+MERGED_EVERY = 2
+BLOCKS_A_STEP = 4
+RESULT_BUFFERS = 16
 SQRT_FLOOR = 2.0**-100
 
 FLOPS = 2 * TOKENS * D_IN * HALVES * HIDDEN
@@ -146,40 +146,80 @@ def tile_linearrtus_t_v_kernel(
             w_codes[quarter], w_scales[quarter] = codes, scales
 
         dz_turned, dz_grouped, dz_codes, dz_scales = {}, {}, {}, {}
+        z_turned, grad_scaled = {}, {}
+
+        def merged(t):
+            return 1 < t < TOKEN_TILES - 1 and t % MERGED_EVERY == 1
+
+        def turn_words(t, words):
+            turned = dz_banks.tile([P, PLANES * HALVES * P], F32, name="dz_turned")
+            for u in range(PLANES):
+                for half in range(HALVES):
+                    nc.tensor.transpose(
+                        turned[:, (u * HALVES + half) * P : (u * HALVES + half + 1) * P],
+                        words[:, half * WORDS + u * P : half * WORDS + (u + 1) * P],
+                        identity[:],
+                    )
+            dz_turned[t] = turned
+
+        def turned_values(t):
+            return dz_turned[t][:].bitcast(BF16).rearrange("p (u c e) -> p c u e", u=PLANES, e=PAIR)
+
+        def turn_z_and_grad(t):
+            turn_words(t, grad_of[t].bitcast(F32))
+            halves = []
+            for half in range(HALVES):
+                turned = banks.tile([P, PACK, P], F32, name="z_turned", tag="bank")
+                for u in range(PLANES):
+                    for e in range(PAIR):
+                        first = half * HIDDEN + u * PAIR * P + e
+                        nc.tensor.transpose(
+                            turned[:, u * PAIR + e, :],
+                            z_of[t][:, first : half * HIDDEN + (u + 1) * PAIR * P : PAIR],
+                            identity[:],
+                        )
+                halves.append(turned)
+            z_turned[t] = halves
+
+        def scale_grad(t):
+            scaled = dz_work.tile([P, PACK, HALVES * P], BF16)
+            values = turned_values(t)
+            for u in range(PLANES):
+                for e in range(PAIR):
+                    nc.scalar.activation(
+                        out=scaled[:, u * PAIR + e, :],
+                        in_=values[:, :, u, e],
+                        func=ACT.Copy,
+                        scale=norm[:, u * PAIR + e : u * PAIR + e + 1],
+                    )
+            grad_scaled[t] = scaled
+
+        def mask_scaled(t):
+            grouped = dz_work.tile([P, HALVES * P, PLANES, PAIR], BF16, name="grouped", align_bytes=64)
+            for half in range(HALVES):
+                tokens = slice(half * P, (half + 1) * P)
+                nc.vector.scalar_tensor_tensor(
+                    out=grouped[:, tokens, :, :].rearrange("p c u e -> p c (u e)"),
+                    in0=z_turned[t][half][:].rearrange("p k c -> p c k"),
+                    scalar=0.0,
+                    in1=grad_scaled[t][:, :, tokens].rearrange("p k c -> p c k"),
+                    op0=ALU.is_gt,
+                    op1=ALU.mult,
+                )
+            dz_grouped[t] = grouped
 
         def mask_and_turn(t):
             masked = dz_work.tile([P, HALVES * HIDDEN], BF16)
             nc.vector.scalar_tensor_tensor(
                 out=masked[:], in0=z_of[t], scalar=0.0, in1=grad_of[t], op0=ALU.is_gt, op1=ALU.mult
             )
-            masked_words = masked[:].bitcast(F32)
-            turned = dz_banks.tile([P, PLANES * HALVES * P], F32, name="dz_turned")
-            for u in range(PLANES):
-                for half in range(HALVES):
-                    nc.tensor.transpose(
-                        turned[:, (u * HALVES + half) * P : (u * HALVES + half + 1) * P],
-                        masked_words[:, half * WORDS + u * P : half * WORDS + (u + 1) * P],
-                        identity[:],
-                    )
-            dz_turned[t] = turned
-
-        def scalar_scales(t):
-            return t > QUARTERS and t % SCALAR_EVERY == 1
+            turn_words(t, masked[:].bitcast(F32))
 
         def scale_by_norm(t):
-            grouped = dz_work.tile([P, HALVES * P, PLANES, PAIR], BF16, align_bytes=64)
-            values = dz_turned[t][:].bitcast(BF16).rearrange("p (u c e) -> p c u e", u=PLANES, e=PAIR)
-            if scalar_scales(t):
-                for u in range(PLANES):
-                    for e in range(PAIR):
-                        nc.scalar.activation(
-                            out=grouped[:, :, u, e],
-                            in_=values[:, :, u, e],
-                            func=ACT.Copy,
-                            scale=norm[:, u * PAIR + e : u * PAIR + e + 1],
-                        )
-            else:
-                nc.vector.tensor_tensor(out=grouped[:], in0=values, in1=norm_for_all_tokens, op=ALU.mult)
+            grouped = dz_work.tile([P, HALVES * P, PLANES, PAIR], BF16, name="grouped", align_bytes=64)
+            nc.vector.tensor_tensor(
+                out=grouped[:], in0=turned_values(t), in1=norm_for_all_tokens, op=ALU.mult
+            )
             dz_grouped[t] = grouped
 
         def quantise_dz(t):
@@ -192,45 +232,55 @@ def tile_linearrtus_t_v_kernel(
             )
             dz_codes[t], dz_scales[t] = codes, scales
 
-        def multiply(t):
-            result = results.tile([P, D_IN], F32)
-            for block in range(COLUMN_BLOCKS):
-                sums = banks.tile([P, N_MOVING], F32, name="sums", tag="bank")
-                for half in range(HALVES):
-                    quarter = block * HALVES + half
-                    tokens = slice(half * P, (half + 1) * P)
-                    nc.tensor.matmul_mx(
-                        out=sums[:],
-                        lhsT=dz_codes[t][:, tokens].bitcast(E5M2_X4),
-                        lhsT_scale=dz_scales[t][:, tokens],
-                        rhs=w_codes[quarter][:].bitcast(E4M3_X4),
-                        rhs_scale=w_scales[quarter][:],
-                        start=(half == 0),
-                        stop=(half == HALVES - 1),
-                    )
-                nc.scalar.copy(out=result[:, block * N_MOVING : (block + 1) * N_MOVING], in_=sums[:])
-            nc.sync.dma_start(out=out_tiles[:, t, :], in_=result[:])
+        result_of = {}
 
-        def steps_to_quantise(t):
-            return 3 if scalar_scales(t) else 2
+        def multiply(t, block):
+            if block == 0:
+                result_of[t] = results.tile([P, D_IN], F32, name="result")
+            result = result_of[t]
+            sums = banks.tile([P, N_MOVING], F32, name="sums", tag="bank")
+            for half in range(HALVES):
+                quarter = block * HALVES + half
+                tokens = slice(half * P, (half + 1) * P)
+                nc.tensor.matmul_mx(
+                    out=sums[:],
+                    lhsT=dz_codes[t][:, tokens].bitcast(E5M2_X4),
+                    lhsT_scale=dz_scales[t][:, tokens],
+                    rhs=w_codes[quarter][:].bitcast(E4M3_X4),
+                    rhs_scale=w_scales[quarter][:],
+                    start=(half == 0),
+                    stop=(half == HALVES - 1),
+                )
+            columns = slice(block * N_MOVING, (block + 1) * N_MOVING)
+            if t == TOKEN_TILES - 1 and block == 0:
+                nc.vector.tensor_copy(out=result[:, columns], in_=sums[:])
+            else:
+                nc.scalar.copy(out=result[:, columns], in_=sums[:])
+            if block < COLUMN_BLOCKS - 1:
+                return
+            nc.sync.dma_start(out=out_tiles[:, t, :], in_=result[:])
 
         waiting = []
         for step in range(TOKEN_TILES + 2):
             if step < TOKEN_TILES:
-                mask_and_turn(step)
-                if scalar_scales(step):
-                    scale_by_norm(step)
+                if merged(step):
+                    turn_z_and_grad(step)
+                    scale_grad(step)
+                else:
+                    mask_and_turn(step)
             if 1 <= step <= QUARTERS:
                 turn_weight_quarter(step - 1)
             if 2 <= step <= QUARTERS + 1:
                 quantise_weight_quarter(step - 2)
-            for t in (step - 3, step - 2):
-                if 0 <= t < TOKEN_TILES and step - t == steps_to_quantise(t):
-                    quantise_dz(t)
-                    waiting.append(t)
-            if 1 <= step <= TOKEN_TILES and not scalar_scales(step - 1):
-                scale_by_norm(step - 1)
-            if step > QUARTERS:
-                for t in waiting[:PRODUCTS_A_STEP]:
-                    multiply(t)
-                waiting = waiting[PRODUCTS_A_STEP:]
+            if step >= 2:
+                quantise_dz(step - 2)
+                waiting += [(step - 2, block) for block in range(COLUMN_BLOCKS)]
+            if 1 <= step <= TOKEN_TILES:
+                if merged(step - 1):
+                    mask_scaled(step - 1)
+                else:
+                    scale_by_norm(step - 1)
+            ready = [(t, block) for t, block in waiting if (block + 1) * HALVES <= len(w_codes)]
+            for t, block in ready[:BLOCKS_A_STEP]:
+                multiply(t, block)
+                waiting.remove((t, block))

@@ -23,10 +23,11 @@ TOKEN_TILES = TOKENS // P
 N_MOVING = 512
 COLUMN_BLOCKS = D_IN // N_MOVING
 QUARTERS = HALVES * COLUMN_BLOCKS
-ROWS_TOGETHER = 2
+ROWS_A_BANK = 2
+ROWS_TOGETHER = N_MOVING // P
 MERGED_EVERY = 2
 BLOCKS_A_STEP = 4
-RESULT_BUFFERS = 16
+STORE_STARTS = (0, 4, 8, 10, 12, 13, 14, 15)
 SQRT_FLOOR = 2.0**-100
 
 FLOPS = 2 * TOKENS * D_IN * HALVES * HIDDEN
@@ -50,7 +51,7 @@ def tile_linearrtus_t_v_kernel(
         w_work = pools.enter_context(tc.tile_pool(name="w_work", bufs=2))
         dz_work = pools.enter_context(tc.tile_pool(name="dz_work", bufs=4))
         dz_keep = pools.enter_context(tc.tile_pool(name="dz_keep", bufs=6))
-        results = pools.enter_context(tc.tile_pool(name="results", bufs=RESULT_BUFFERS))
+        results = pools.enter_context(tc.tile_pool(name="results", bufs=1))
         dz_banks = pools.enter_context(tc.psum_pool(name="dz_banks", bufs=2))
         banks = pools.enter_context(tc.psum_pool(name="banks", bufs=6))
 
@@ -68,12 +69,8 @@ def tile_linearrtus_t_v_kernel(
         def load_weight_quarter(quarter):
             block, half = divmod(quarter, HALVES)
             rows = weights[half][block * N_MOVING : (block + 1) * N_MOVING, :]
-            w_sb = loaded.tile(
-                [P, N_MOVING // (P * ROWS_TOGETHER), ROWS_TOGETHER, HIDDEN], BF16, name="w%d" % quarter
-            )
-            nc.sync.dma_start(
-                out=w_sb[:], in_=rows.rearrange("(j c i) k -> c j i k", c=P, i=ROWS_TOGETHER)
-            )
+            w_sb = loaded.tile([P, ROWS_TOGETHER, HIDDEN], BF16, name="w%d" % quarter)
+            nc.sync.dma_start(out=w_sb[:], in_=rows.rearrange("(c i) k -> c i k", i=ROWS_TOGETHER))
             w_rows[quarter] = w_sb
 
         r_sb = const.tile([P, PACK], BF16)
@@ -117,23 +114,20 @@ def tile_linearrtus_t_v_kernel(
 
         def turn_weight_quarter(quarter):
             grouped = w_work.tile([P, N_MOVING * PACK], BF16, name="w_grouped", align_bytes=64)
-            grouped_words = grouped[:].bitcast(F32)
-            per_bank = P * ROWS_TOGETHER
-            for j in range(N_MOVING // per_bank):
-                turned = banks.tile([P, PLANES * per_bank], F32, name="w_turned", tag="bank")
+            grouped_words = grouped[:].bitcast(F32).rearrange(
+                "p (c i u) -> p c i u", i=ROWS_TOGETHER, u=PLANES
+            )
+            for i in range(0, ROWS_TOGETHER, ROWS_A_BANK):
+                turned = banks.tile([P, PLANES, ROWS_A_BANK, P], F32, name="w_turned", tag="bank")
                 for u in range(PLANES):
-                    for i in range(ROWS_TOGETHER):
-                        row_words = w_rows[quarter][:, j, i, :].bitcast(F32)
+                    for n in range(ROWS_A_BANK):
+                        row_words = w_rows[quarter][:, i + n, :].bitcast(F32)
                         nc.tensor.transpose(
-                            turned[:, (u * ROWS_TOGETHER + i) * P : (u * ROWS_TOGETHER + i + 1) * P],
-                            row_words[:, u * P : (u + 1) * P],
-                            identity[:],
+                            turned[:, u, n, :], row_words[:, u * P : (u + 1) * P], identity[:]
                         )
                 nc.scalar.copy(
-                    out=grouped_words[:, j * per_bank * PLANES : (j + 1) * per_bank * PLANES].rearrange(
-                        "p (c i u) -> p c i u", i=ROWS_TOGETHER, u=PLANES
-                    ),
-                    in_=turned[:].rearrange("p (u i c) -> p c i u", u=PLANES, i=ROWS_TOGETHER),
+                    out=grouped_words[:, :, i : i + ROWS_A_BANK, :],
+                    in_=turned[:].rearrange("p u i c -> p c i u"),
                 )
             w_grouped[quarter] = grouped
 
@@ -235,9 +229,12 @@ def tile_linearrtus_t_v_kernel(
         result_of = {}
 
         def multiply(t, block):
-            if block == 0:
-                result_of[t] = results.tile([P, D_IN], F32, name="result")
-            result = result_of[t]
+            first = max(start for start in STORE_STARTS if start <= t)
+            if block == 0 and t == first:
+                after = min([start for start in STORE_STARTS if start > t] + [TOKEN_TILES])
+                result_of[first] = results.tile([P, after - first, D_IN], F32, name="result%d" % first)
+            stored = result_of[first]
+            result = stored[:, t - first, :]
             sums = banks.tile([P, N_MOVING], F32, name="sums", tag="bank")
             for half in range(HALVES):
                 quarter = block * HALVES + half
@@ -256,9 +253,9 @@ def tile_linearrtus_t_v_kernel(
                 nc.vector.tensor_copy(out=result[:, columns], in_=sums[:])
             else:
                 nc.scalar.copy(out=result[:, columns], in_=sums[:])
-            if block < COLUMN_BLOCKS - 1:
-                return
-            nc.sync.dma_start(out=out_tiles[:, t, :], in_=result[:])
+            count = stored.shape[1]
+            if block == COLUMN_BLOCKS - 1 and t == first + count - 1:
+                nc.sync.dma_start(out=out_tiles[:, first : first + count, :], in_=stored[:])
 
         waiting = []
         for step in range(TOKEN_TILES + 2):

@@ -57,14 +57,17 @@ def tile_linearrtus_t_v_kernel(
 
         z_of, grad_of, w_rows = {}, {}, {}
 
-        def load_tokens(first, count):
-            grad_sb = loaded.tile([P, count, HALVES * HIDDEN], BF16, name="grad%d" % first)
+        def load_z(first, count):
             z_sb = loaded.tile([P, count, HALVES * HIDDEN], F32, name="z%d" % first)
-            nc.sync.dma_start(out=grad_sb[:], in_=grad_tiles[:, first : first + count, :])
             nc.sync.dma_start(out=z_sb[:], in_=z_tiles[:, first : first + count, :])
             for n in range(count):
-                grad_of[first + n] = grad_sb[:, n, :]
                 z_of[first + n] = z_sb[:, n, :]
+
+        def load_grad(first, count):
+            grad_sb = loaded.tile([P, count, HALVES * HIDDEN], BF16, name="grad%d" % first)
+            nc.sync.dma_start(out=grad_sb[:], in_=grad_tiles[:, first : first + count, :])
+            for n in range(count):
+                grad_of[first + n] = grad_sb[:, n, :]
 
         def load_weight_quarter(quarter):
             block, half = divmod(quarter, HALVES)
@@ -78,13 +81,20 @@ def tile_linearrtus_t_v_kernel(
             out=r_sb[:].rearrange("p (u e) -> p u e", e=PAIR),
             in_=r_param.rearrange("o (u p e) -> p (o u) e", u=PLANES, e=PAIR),
         )
-        load_tokens(0, 1)
+        load_grad(0, 1)
+        load_z(0, 1)
         for quarter in range(QUARTERS):
-            load_tokens(quarter + 1, 1)
+            if quarter % 2 == 0:
+                load_grad(quarter + 1, 2)
+            load_z(quarter + 1, 1)
             load_weight_quarter(quarter)
-        for first in range(QUARTERS + 1, TOKEN_TILES - 1, 2):
-            load_tokens(first, 2)
-        load_tokens(TOKEN_TILES - 1, 1)
+        load_grad(5, 4)
+        load_z(5, 2)
+        load_z(7, 2)
+        load_grad(9, 4)
+        load_z(9, 4)
+        load_grad(13, 3)
+        load_z(13, 3)
 
         identity = const.tile([P, P], F32)
         make_identity(nc, identity[:])

@@ -25,7 +25,7 @@ COLUMN_BLOCKS = D_IN // N_MOVING
 QUARTERS = HALVES * COLUMN_BLOCKS
 ROWS_A_BANK = 2
 ROWS_TOGETHER = N_MOVING // P
-MERGED_EVERY = 2
+MERGED_EVERY = 3
 BLOCKS_A_STEP = 4
 STORE_STARTS = (0, 4, 8, 10, 12, 13, 14, 15)
 SQRT_FLOOR = 2.0**-100
@@ -84,15 +84,18 @@ def tile_linearrtus_t_v_kernel(
         load_grad(0, 1)
         load_z(0, 1)
         for quarter in range(QUARTERS):
-            if quarter % 2 == 0:
+            if quarter < 2:
+                load_grad(quarter + 1, 1)
+            if quarter == 2:
                 load_grad(quarter + 1, 2)
             load_z(quarter + 1, 1)
             load_weight_quarter(quarter)
-        load_grad(5, 4)
-        load_z(5, 2)
-        load_z(7, 2)
+        for first in (5, 7):
+            load_grad(first, 2)
+            load_z(first, 2)
         load_grad(9, 4)
-        load_z(9, 4)
+        load_z(9, 2)
+        load_z(11, 2)
         load_grad(13, 3)
         load_z(13, 3)
 
@@ -153,7 +156,7 @@ def tile_linearrtus_t_v_kernel(
         z_turned, grad_scaled = {}, {}
 
         def merged(t):
-            return 1 < t < TOKEN_TILES - 1 and t % MERGED_EVERY == 1
+            return t % MERGED_EVERY == MERGED_EVERY - 1 and t < TOKEN_TILES - 1
 
         def turn_words(t, words):
             turned = dz_banks.tile([P, PLANES * HALVES * P], F32, name="dz_turned")

@@ -27,7 +27,7 @@ ROWS_A_BANK = 2
 ROWS_TOGETHER = N_MOVING // P
 MERGED_EVERY = 3
 BLOCKS_A_STEP = 4
-STORE_STARTS = (0, 4, 8, 10, 12, 13, 14, 15)
+STORE_STARTS = (0, 4, 8, 10, 12, 14, 15)
 SQRT_FLOOR = 2.0**-100
 
 FLOPS = 2 * TOKENS * D_IN * HALVES * HIDDEN
@@ -76,10 +76,10 @@ def tile_linearrtus_t_v_kernel(
             nc.sync.dma_start(out=w_sb[:], in_=rows.rearrange("(c i) k -> c i k", i=ROWS_TOGETHER))
             w_rows[quarter] = w_sb
 
-        r_sb = const.tile([P, PACK], BF16)
+        r_rows = const.tile([P, P], F32)
+        nc.gpsimd.memset(r_rows[:], 0.0)
         nc.scalar.dma_start(
-            out=r_sb[:].rearrange("p (u e) -> p u e", e=PAIR),
-            in_=r_param.rearrange("o (u p e) -> p (o u) e", u=PLANES, e=PAIR),
+            out=r_rows[:PLANES, :].bitcast(BF16), in_=r_param.rearrange("o (u k) -> (o u) k", u=PLANES)
         )
         load_grad(0, 1)
         load_z(0, 1)
@@ -102,20 +102,27 @@ def tile_linearrtus_t_v_kernel(
         identity = const.tile([P, P], F32)
         make_identity(nc, identity[:])
 
-        r_squared = const.tile([P, PACK], F32)
-        nc.vector.tensor_tensor(out=r_squared[:], in0=r_sb[:], in1=r_sb[:], op=ALU.mult)
-        one_minus = const.tile([P, PACK], F32)
-        nc.vector.tensor_scalar(
-            out=one_minus[:], in0=r_squared[:], scalar1=-1.0, scalar2=1.0, op0=ALU.mult, op1=ALU.add
-        )
-        floored = const.tile([P, PACK], F32)
-        nc.vector.tensor_scalar_max(out=floored[:], in0=one_minus[:], scalar1=SQRT_FLOOR)
-        root = const.tile([P, PACK], F32)
-        nc.scalar.activation(out=root[:], in_=floored[:], func=ACT.Sqrt)
+        r_turned = banks.tile([P, P], F32, name="r_turned", tag="bank")
+        nc.tensor.transpose(r_turned[:], r_rows[:], identity[:])
         norm = const.tile([P, PACK], F32)
-        nc.vector.scalar_tensor_tensor(
-            out=norm[:], in0=one_minus[:], scalar=0.0, in1=root[:], op0=ALU.is_gt, op1=ALU.mult
-        )
+
+        def compute_norm():
+            r_sb = const.tile([P, PACK], BF16)
+            nc.vector.tensor_copy(out=r_sb[:], in_=r_turned[:, :PLANES].bitcast(BF16))
+            r_squared = const.tile([P, PACK], F32)
+            nc.vector.tensor_tensor(out=r_squared[:], in0=r_sb[:], in1=r_sb[:], op=ALU.mult)
+            one_minus = const.tile([P, PACK], F32)
+            nc.vector.tensor_scalar(
+                out=one_minus[:], in0=r_squared[:], scalar1=-1.0, scalar2=1.0, op0=ALU.mult, op1=ALU.add
+            )
+            floored = const.tile([P, PACK], F32)
+            nc.vector.tensor_scalar_max(out=floored[:], in0=one_minus[:], scalar1=SQRT_FLOOR)
+            root = const.tile([P, PACK], F32)
+            nc.scalar.activation(out=root[:], in_=floored[:], func=ACT.Sqrt)
+            nc.vector.scalar_tensor_tensor(
+                out=norm[:], in0=one_minus[:], scalar=0.0, in1=root[:], op0=ALU.is_gt, op1=ALU.mult
+            )
+
         norm_for_all_tokens = (
             norm[:]
             .rearrange("p (u e) -> p u e", e=PAIR)
@@ -156,7 +163,7 @@ def tile_linearrtus_t_v_kernel(
         z_turned, grad_scaled = {}, {}
 
         def merged(t):
-            return t % MERGED_EVERY == MERGED_EVERY - 1 and t < TOKEN_TILES - 1
+            return t > QUARTERS and t % MERGED_EVERY == MERGED_EVERY - 1 and t < TOKEN_TILES - 1
 
         def turn_words(t, words):
             turned = dz_banks.tile([P, PLANES * HALVES * P], F32, name="dz_turned")
@@ -278,10 +285,10 @@ def tile_linearrtus_t_v_kernel(
                     scale_grad(step)
                 else:
                     mask_and_turn(step)
+            if step == 0:
+                compute_norm()
             if 1 <= step <= QUARTERS:
                 turn_weight_quarter(step - 1)
-            if 2 <= step <= QUARTERS + 1:
-                quantise_weight_quarter(step - 2)
             if step >= 2:
                 quantise_dz(step - 2)
                 waiting += [(step - 2, block) for block in range(COLUMN_BLOCKS)]
@@ -290,6 +297,8 @@ def tile_linearrtus_t_v_kernel(
                     mask_scaled(step - 1)
                 else:
                     scale_by_norm(step - 1)
+            if 2 <= step <= QUARTERS + 1:
+                quantise_weight_quarter(step - 2)
             ready = [(t, block) for t, block in waiting if (block + 1) * HALVES <= len(w_codes)]
             for t, block in ready[:BLOCKS_A_STEP]:
                 multiply(t, block)

@@ -19,6 +19,7 @@ PLANES = 2
 PAIR = 2
 PACK = PLANES * PAIR
 WORDS = HIDDEN // PAIR
+GROUP = 4
 TOKEN_TILES = TOKENS // P
 N_MOVING = 512
 COLUMN_BLOCKS = D_IN // N_MOVING
@@ -39,9 +40,13 @@ def tile_linearrtus_t_v_kernel(
 ):
     nc = tc.nc
     weights = (w1, w2)
-    z_tiles = z.rearrange("(p t) k -> p t k", t=TOKEN_TILES)
-    grad_tiles = grad_out.rearrange("(p t) k -> p t k", t=TOKEN_TILES)
-    out_tiles = out.rearrange("(p t) d -> p t d", t=TOKEN_TILES)
+    z_tiles = z.rearrange("(g p i) k -> p g i k", p=P, i=GROUP)
+    grad_tiles = grad_out.rearrange("(g p i) k -> p g i k", p=P, i=GROUP)
+    out_tiles = out.rearrange("(g p i) d -> p g i d", p=P, i=GROUP)
+
+    def in_group(tiles, first, count):
+        group, member = divmod(first, GROUP)
+        return tiles[:, group, member : member + count, :]
 
     with ExitStack() as pools:
         pools.enter_context(tc.manual_schedule())
@@ -59,13 +64,13 @@ def tile_linearrtus_t_v_kernel(
 
         def load_z(first, count):
             z_sb = loaded.tile([P, count, HALVES * HIDDEN], F32, name="z%d" % first)
-            nc.sync.dma_start(out=z_sb[:], in_=z_tiles[:, first : first + count, :])
+            nc.sync.dma_start(out=z_sb[:], in_=in_group(z_tiles, first, count))
             for n in range(count):
                 z_of[first + n] = z_sb[:, n, :]
 
         def load_grad(first, count):
             grad_sb = loaded.tile([P, count, HALVES * HIDDEN], BF16, name="grad%d" % first)
-            nc.sync.dma_start(out=grad_sb[:], in_=grad_tiles[:, first : first + count, :])
+            nc.sync.dma_start(out=grad_sb[:], in_=in_group(grad_tiles, first, count))
             for n in range(count):
                 grad_of[first + n] = grad_sb[:, n, :]
 
@@ -84,20 +89,21 @@ def tile_linearrtus_t_v_kernel(
         load_grad(0, 1)
         load_z(0, 1)
         for quarter in range(QUARTERS):
-            if quarter < 2:
-                load_grad(quarter + 1, 1)
-            if quarter == 2:
-                load_grad(quarter + 1, 2)
-            load_z(quarter + 1, 1)
+            t = quarter + 1
+            if t == 1:
+                load_grad(t, 1)
+            elif t % 2 == 0:
+                load_grad(t, 2)
+            load_z(t, 1)
             load_weight_quarter(quarter)
-        for first in (5, 7):
-            load_grad(first, 2)
-            load_z(first, 2)
-        load_grad(9, 4)
-        load_z(9, 2)
-        load_z(11, 2)
-        load_grad(13, 3)
-        load_z(13, 3)
+        load_z(5, 1)
+        load_grad(6, 2)
+        load_z(6, 2)
+        load_grad(8, 4)
+        load_z(8, 2)
+        load_z(10, 2)
+        load_grad(12, 4)
+        load_z(12, 4)
 
         identity = const.tile([P, P], F32)
         make_identity(nc, identity[:])
@@ -275,7 +281,7 @@ def tile_linearrtus_t_v_kernel(
                 nc.scalar.copy(out=result[:, columns], in_=sums[:])
             count = stored.shape[1]
             if block == COLUMN_BLOCKS - 1 and t == first + count - 1:
-                nc.sync.dma_start(out=out_tiles[:, first : first + count, :], in_=stored[:])
+                nc.sync.dma_start(out=in_group(out_tiles, first, count), in_=stored[:])
 
         waiting = []
         for step in range(TOKEN_TILES + 2):

@@ -28,7 +28,8 @@ ROWS_A_BANK = 2
 ROWS_TOGETHER = N_MOVING // P
 MERGED_EVERY = 3
 BLOCKS_A_STEP = 4
-STORE_STARTS = (0, 4, 8, 10, 12, 14, 15)
+STORE_STARTS = (0, 4) + tuple(range(8, TOKEN_TILES))
+DMA_ALIGN = 256
 SQRT_FLOOR = 2.0**-100
 
 FLOPS = 2 * TOKENS * D_IN * HALVES * HIDDEN
@@ -63,13 +64,13 @@ def tile_linearrtus_t_v_kernel(
         z_of, grad_of, w_rows = {}, {}, {}
 
         def load_z(first, count):
-            z_sb = loaded.tile([P, count, HALVES * HIDDEN], F32, name="z%d" % first)
+            z_sb = loaded.tile([P, count, HALVES * HIDDEN], F32, name="z%d" % first, align_bytes=DMA_ALIGN)
             nc.sync.dma_start(out=z_sb[:], in_=in_group(z_tiles, first, count))
             for n in range(count):
                 z_of[first + n] = z_sb[:, n, :]
 
         def load_grad(first, count):
-            grad_sb = loaded.tile([P, count, HALVES * HIDDEN], BF16, name="grad%d" % first)
+            grad_sb = loaded.tile([P, count, HALVES * HIDDEN], BF16, name="grad%d" % first, align_bytes=DMA_ALIGN)
             nc.sync.dma_start(out=grad_sb[:], in_=in_group(grad_tiles, first, count))
             for n in range(count):
                 grad_of[first + n] = grad_sb[:, n, :]
@@ -77,7 +78,7 @@ def tile_linearrtus_t_v_kernel(
         def load_weight_quarter(quarter):
             block, half = divmod(quarter, HALVES)
             rows = weights[half][block * N_MOVING : (block + 1) * N_MOVING, :]
-            w_sb = loaded.tile([P, ROWS_TOGETHER, HIDDEN], BF16, name="w%d" % quarter)
+            w_sb = loaded.tile([P, ROWS_TOGETHER, HIDDEN], BF16, name="w%d" % quarter, align_bytes=DMA_ALIGN)
             nc.sync.dma_start(out=w_sb[:], in_=rows.rearrange("(c i) k -> c i k", i=ROWS_TOGETHER))
             w_rows[quarter] = w_sb
 
@@ -258,7 +259,7 @@ def tile_linearrtus_t_v_kernel(
             first = max(start for start in STORE_STARTS if start <= t)
             if block == 0 and t == first:
                 after = min([start for start in STORE_STARTS if start > t] + [TOKEN_TILES])
-                result_of[first] = results.tile([P, after - first, D_IN], F32, name="result%d" % first)
+                result_of[first] = results.tile([P, after - first, D_IN], F32, name="result%d" % first, align_bytes=DMA_ALIGN)
             stored = result_of[first]
             result = stored[:, t - first, :]
             sums = banks.tile([P, N_MOVING], F32, name="sums", tag="bank")
@@ -280,7 +281,11 @@ def tile_linearrtus_t_v_kernel(
             else:
                 nc.scalar.copy(out=result[:, columns], in_=sums[:])
             count = stored.shape[1]
-            if block == COLUMN_BLOCKS - 1 and t == first + count - 1:
+            if t == TOKEN_TILES - 1:
+                nc.sync.dma_start(
+                    out=in_group(out_tiles, first, count)[:, :, columns], in_=stored[:, :, columns]
+                )
+            elif block == COLUMN_BLOCKS - 1 and t == first + count - 1:
                 nc.sync.dma_start(out=in_group(out_tiles, first, count), in_=stored[:])
 
         waiting = []

from contextlib import ExitStack

import concourse.mybir as mybir
from concourse.masks import make_identity

F32 = mybir.dt.float32
BF16 = mybir.dt.bfloat16
U32 = mybir.dt.uint32
U8 = mybir.dt.uint8
E4M3_X4 = mybir.dt.float8_e4m3fn_x4
E5M2_X4 = mybir.dt.float8_e5m2_x4
ALU = mybir.AluOpType
ACT = mybir.ActivationFunctionType

P = 128
TOKENS, D_IN, HIDDEN = 2048, 1024, 512
HALVES = 2
PLANES = 2
PAIR = 2
PACK = PLANES * PAIR
WORDS = HIDDEN // PAIR
GROUP = 4
TOKEN_TILES = TOKENS // P
N_MOVING = 512
COLUMN_BLOCKS = D_IN // N_MOVING
QUARTERS = HALVES * COLUMN_BLOCKS
ROWS_A_BANK = 2
ROWS_TOGETHER = N_MOVING // P
MERGED_EVERY = 3
BLOCKS_A_STEP = 4
STORE_STARTS = (0, 4) + tuple(range(8, TOKEN_TILES))
DMA_ALIGN = 256
SQRT_FLOOR = 2.0**-100

FLOPS = 2 * TOKENS * D_IN * HALVES * HIDDEN
BYTES = 2 * HIDDEN + 2 * HALVES * D_IN * HIDDEN + (4 + 2) * TOKENS * HALVES * HIDDEN + 4 * TOKENS * D_IN


def tile_linearrtus_t_v_kernel(
    tc, h_c1, h_c2, x_t, r_param, theta_param, w1, w2, z, grad_out, out
):
    nc = tc.nc
    weights = (w1, w2)
    z_tiles = z.rearrange("(g p i) k -> p g i k", p=P, i=GROUP)
    grad_tiles = grad_out.rearrange("(g p i) k -> p g i k", p=P, i=GROUP)
    out_tiles = out.rearrange("(g p i) d -> p g i d", p=P, i=GROUP)

    def in_group(tiles, first, count):
        group, member = divmod(first, GROUP)
        return tiles[:, group, member : member + count, :]

    with ExitStack() as pools:
        pools.enter_context(tc.manual_schedule())
        const = pools.enter_context(tc.tile_pool(name="const", bufs=1))
        loaded = pools.enter_context(tc.tile_pool(name="loaded", bufs=1))
        w_keep = pools.enter_context(tc.tile_pool(name="w_keep", bufs=1))
        w_work = pools.enter_context(tc.tile_pool(name="w_work", bufs=2))
        dz_work = pools.enter_context(tc.tile_pool(name="dz_work", bufs=4))
        dz_keep = pools.enter_context(tc.tile_pool(name="dz_keep", bufs=6))
        results = pools.enter_context(tc.tile_pool(name="results", bufs=1))
        dz_banks = pools.enter_context(tc.psum_pool(name="dz_banks", bufs=2))
        banks = pools.enter_context(tc.psum_pool(name="banks", bufs=6))

        z_of, grad_of, w_rows = {}, {}, {}

        def load_z(first, count):
            z_sb = loaded.tile([P, count, HALVES * HIDDEN], F32, name="z%d" % first, align_bytes=DMA_ALIGN)
            nc.sync.dma_start(out=z_sb[:], in_=in_group(z_tiles, first, count))
            for n in range(count):
                z_of[first + n] = z_sb[:, n, :]

        def load_grad(first, count):
            grad_sb = loaded.tile([P, count, HALVES * HIDDEN], BF16, name="grad%d" % first, align_bytes=DMA_ALIGN)
            nc.sync.dma_start(out=grad_sb[:], in_=in_group(grad_tiles, first, count))
            for n in range(count):
                grad_of[first + n] = grad_sb[:, n, :]

        def load_weight_quarter(quarter):
            block, half = divmod(quarter, HALVES)
            rows = weights[half][block * N_MOVING : (block + 1) * N_MOVING, :]
            w_sb = loaded.tile([P, ROWS_TOGETHER, HIDDEN], BF16, name="w%d" % quarter, align_bytes=DMA_ALIGN)
            nc.sync.dma_start(out=w_sb[:], in_=rows.rearrange("(c i) k -> c i k", i=ROWS_TOGETHER))
            w_rows[quarter] = w_sb

        r_rows = const.tile([P, P], F32)
        nc.gpsimd.memset(r_rows[:], 0.0)
        nc.scalar.dma_start(
            out=r_rows[:PLANES, :].bitcast(BF16), in_=r_param.rearrange("o (u k) -> (o u) k", u=PLANES)
        )
        load_grad(0, 1)
        load_z(0, 1)
        for quarter in range(QUARTERS):
            t = quarter + 1
            if t == 1:
                load_grad(t, 1)
            elif t % 2 == 0:
                load_grad(t, 2)
            load_z(t, 1)
            load_weight_quarter(quarter)
        load_z(5, 1)
        load_grad(6, 2)
        load_z(6, 2)
        load_grad(8, 4)
        load_z(8, 2)
        load_z(10, 2)
        load_grad(12, 4)
        load_z(12, 4)

        identity = const.tile([P, P], F32)
        make_identity(nc, identity[:])

        r_turned = banks.tile([P, P], F32, name="r_turned", tag="bank")
        nc.tensor.transpose(r_turned[:], r_rows[:], identity[:])
        norm = const.tile([P, PACK], F32)

        def compute_norm():
            r_sb = const.tile([P, PACK], BF16)
            nc.vector.tensor_copy(out=r_sb[:], in_=r_turned[:, :PLANES].bitcast(BF16))
            r_squared = const.tile([P, PACK], F32)
            nc.vector.tensor_tensor(out=r_squared[:], in0=r_sb[:], in1=r_sb[:], op=ALU.mult)
            one_minus = const.tile([P, PACK], F32)
            nc.vector.tensor_scalar(
                out=one_minus[:], in0=r_squared[:], scalar1=-1.0, scalar2=1.0, op0=ALU.mult, op1=ALU.add
            )
            floored = const.tile([P, PACK], F32)
            nc.vector.tensor_scalar_max(out=floored[:], in0=one_minus[:], scalar1=SQRT_FLOOR)
            root = const.tile([P, PACK], F32)
            nc.scalar.activation(out=root[:], in_=floored[:], func=ACT.Sqrt)
            nc.vector.scalar_tensor_tensor(
                out=norm[:], in0=one_minus[:], scalar=0.0, in1=root[:], op0=ALU.is_gt, op1=ALU.mult
            )

        norm_for_all_tokens = (
            norm[:]
            .rearrange("p (u e) -> p u e", e=PAIR)
            .unsqueeze(1)
            .to_broadcast([P, HALVES * P, PLANES, PAIR])
        )

        w_grouped, w_codes, w_scales = {}, {}, {}

        def turn_weight_quarter(quarter):
            grouped = w_work.tile([P, N_MOVING * PACK], BF16, name="w_grouped", align_bytes=64)
            grouped_words = grouped[:].bitcast(F32).rearrange(
                "p (c i u) -> p c i u", i=ROWS_TOGETHER, u=PLANES
            )
            for i in range(0, ROWS_TOGETHER, ROWS_A_BANK):
                turned = banks.tile([P, PLANES, ROWS_A_BANK, P], F32, name="w_turned", tag="bank")
                for u in range(PLANES):
                    for n in range(ROWS_A_BANK):
                        row_words = w_rows[quarter][:, i + n, :].bitcast(F32)
                        nc.tensor.transpose(
                            turned[:, u, n, :], row_words[:, u * P : (u + 1) * P], identity[:]
                        )
                nc.scalar.copy(
                    out=grouped_words[:, :, i : i + ROWS_A_BANK, :],
                    in_=turned[:].rearrange("p u i c -> p c i u"),
                )
            w_grouped[quarter] = grouped

        def quantise_weight_quarter(quarter):
            codes = w_keep.tile([P, N_MOVING], U32, name="w_codes%d" % quarter, align_bytes=64)
            scales = w_keep.tile([P, N_MOVING], U8, name="w_scales%d" % quarter, align_bytes=64)
            nc.vector.quantize_mx(
                out=codes[:].bitcast(E4M3_X4), scales=scales[:], in_=w_grouped[quarter][:]
            )
            w_codes[quarter], w_scales[quarter] = codes, scales

        dz_turned, dz_grouped, dz_codes, dz_scales = {}, {}, {}, {}
        z_turned, grad_scaled = {}, {}

        def merged(t):
            return t > QUARTERS and t % MERGED_EVERY == MERGED_EVERY - 1 and t < TOKEN_TILES - 1

        def turn_words(t, words):
            turned = dz_banks.tile([P, PLANES * HALVES * P], F32, name="dz_turned")
            for u in range(PLANES):
                for half in range(HALVES):
                    nc.tensor.transpose(
                        turned[:, (u * HALVES + half) * P : (u * HALVES + half + 1) * P],
                        words[:, half * WORDS + u * P : half * WORDS + (u + 1) * P],
                        identity[:],
                    )
            dz_turned[t] = turned

        def turned_values(t):
            return dz_turned[t][:].bitcast(BF16).rearrange("p (u c e) -> p c u e", u=PLANES, e=PAIR)

        def turn_z_and_grad(t):
            turn_words(t, grad_of[t].bitcast(F32))
            halves = []
            for half in range(HALVES):
                turned = banks.tile([P, PACK, P], F32, name="z_turned", tag="bank")
                for u in range(PLANES):
                    for e in range(PAIR):
                        first = half * HIDDEN + u * PAIR * P + e
                        nc.tensor.transpose(
                            turned[:, u * PAIR + e, :],
                            z_of[t][:, first : half * HIDDEN + (u + 1) * PAIR * P : PAIR],
                            identity[:],
                        )
                halves.append(turned)
            z_turned[t] = halves

        def scale_grad(t):
            scaled = dz_work.tile([P, PACK, HALVES * P], BF16)
            values = turned_values(t)
            for u in range(PLANES):
                for e in range(PAIR):
                    nc.scalar.activation(
                        out=scaled[:, u * PAIR + e, :],
                        in_=values[:, :, u, e],
                        func=ACT.Copy,
                        scale=norm[:, u * PAIR + e : u * PAIR + e + 1],
                    )
            grad_scaled[t] = scaled

        def mask_scaled(t):
            grouped = dz_work.tile([P, HALVES * P, PLANES, PAIR], BF16, name="grouped", align_bytes=64)
            for half in range(HALVES):
                tokens = slice(half * P, (half + 1) * P)
                nc.vector.scalar_tensor_tensor(
                    out=grouped[:, tokens, :, :].rearrange("p c u e -> p c (u e)"),
                    in0=z_turned[t][half][:].rearrange("p k c -> p c k"),
                    scalar=0.0,
                    in1=grad_scaled[t][:, :, tokens].rearrange("p k c -> p c k"),
                    op0=ALU.is_gt,
                    op1=ALU.mult,
                )
            dz_grouped[t] = grouped

        def mask_and_turn(t):
            masked = dz_work.tile([P, HALVES * HIDDEN], BF16)
            nc.vector.scalar_tensor_tensor(
                out=masked[:], in0=z_of[t], scalar=0.0, in1=grad_of[t], op0=ALU.is_gt, op1=ALU.mult
            )
            turn_words(t, masked[:].bitcast(F32))

        def scale_by_norm(t):
            grouped = dz_work.tile([P, HALVES * P, PLANES, PAIR], BF16, name="grouped", align_bytes=64)
            nc.vector.tensor_tensor(
                out=grouped[:], in0=turned_values(t), in1=norm_for_all_tokens, op=ALU.mult
            )
            dz_grouped[t] = grouped

        def quantise_dz(t):
            codes = dz_keep.tile([P, HALVES * P], U32, name="dz_codes", align_bytes=64)
            scales = dz_keep.tile([P, HALVES * P], U8, name="dz_scales", align_bytes=64)
            nc.vector.quantize_mx(
                out=codes[:].bitcast(E5M2_X4),
                scales=scales[:],
                in_=dz_grouped[t][:].rearrange("p c u e -> p (c u e)"),
            )
            dz_codes[t], dz_scales[t] = codes, scales

        result_of = {}

        def multiply(t, block):
            first = max(start for start in STORE_STARTS if start <= t)
            if block == 0 and t == first:
                after = min([start for start in STORE_STARTS if start > t] + [TOKEN_TILES])
                result_of[first] = results.tile([P, after - first, D_IN], F32, name="result%d" % first, align_bytes=DMA_ALIGN)
            stored = result_of[first]
            result = stored[:, t - first, :]
            sums = banks.tile([P, N_MOVING], F32, name="sums", tag="bank")
            for half in range(HALVES):
                quarter = block * HALVES + half
                tokens = slice(half * P, (half + 1) * P)
                nc.tensor.matmul_mx(
                    out=sums[:],
                    lhsT=dz_codes[t][:, tokens].bitcast(E5M2_X4),
                    lhsT_scale=dz_scales[t][:, tokens],
                    rhs=w_codes[quarter][:].bitcast(E4M3_X4),
                    rhs_scale=w_scales[quarter][:],
                    start=(half == 0),
                    stop=(half == HALVES - 1),
                )
            columns = slice(block * N_MOVING, (block + 1) * N_MOVING)
            if t == TOKEN_TILES - 1 and block == 0:
                nc.vector.tensor_copy(out=result[:, columns], in_=sums[:])
            else:
                nc.scalar.copy(out=result[:, columns], in_=sums[:])
            count = stored.shape[1]
            if t == TOKEN_TILES - 1:
                nc.sync.dma_start(
                    out=in_group(out_tiles, first, count)[:, :, columns], in_=stored[:, :, columns]
                )
            elif block == COLUMN_BLOCKS - 1 and t == first + count - 1:
                nc.sync.dma_start(out=in_group(out_tiles, first, count), in_=stored[:])

        waiting = []
        for step in range(TOKEN_TILES + 2):
            if step < TOKEN_TILES:
                if merged(step):
                    turn_z_and_grad(step)
                    scale_grad(step)
                else:
                    mask_and_turn(step)
            if step == 0:
                compute_norm()
            if 1 <= step <= QUARTERS:
                turn_weight_quarter(step - 1)
            if step >= 2:
                quantise_dz(step - 2)
                waiting += [(step - 2, block) for block in range(COLUMN_BLOCKS)]
            if 1 <= step <= TOKEN_TILES:
                if merged(step - 1):
                    mask_scaled(step - 1)
                else:
                    scale_by_norm(step - 1)
            if 2 <= step <= QUARTERS + 1:
                quantise_weight_quarter(step - 2)
            ready = [(t, block) for t, block in waiting if (block + 1) * HALVES <= len(w_codes)]
            for t, block in ready[:BLOCKS_A_STEP]:
                multiply(t, block)
                waiting.remove((t, block))
